import numpy as np
import ml_dtypes


def mxq(x, axis, fmt="e4m3"):
    dtype, down = {"e4m3": (ml_dtypes.float8_e4m3fn, 7), "e5m2": (ml_dtypes.float8_e5m2, 14)}[fmt]
    v = np.moveaxis(np.asarray(x, np.float32).astype(ml_dtypes.bfloat16).astype(np.float64), axis, -1)
    blocks = v.reshape(v.shape[:-1] + (-1, 32))
    amax = np.abs(blocks).max(-1, keepdims=True)
    byte = np.maximum(np.where(amax > 0, np.frexp(amax)[1] - 1 + 127, 0) - down, 1)
    scale = np.exp2(byte - 127.0)
    codes = (blocks / scale).astype(np.float32).astype(dtype).astype(np.float64)
    return np.moveaxis((codes * scale).reshape(v.shape), -1, axis)


WIDE = False


def mx_kscale(k):
    if not WIDE:
        return np.ones(k)
    levels = np.array([10, -10, 5, -5, 0])
    a = np.random.permutation(np.resize(levels, k // 512 * 4)).reshape(k // 512, 4)
    idx = np.arange(k)
    return np.exp2(a[idx // 512, idx % 128 // 32])


BF16 = ml_dtypes.bfloat16


def bf(x):
    return np.asarray(x, np.float32).astype(BF16)


def f64(x):
    return np.asarray(x).astype(np.float64)


B, CL, CH, CK, CV, CO, H, W = 2, 1024, 2048, 256, 512, 1024, 24, 24
N = H * W
CF = CO + CH
EPS = 1e-5


def setup_inputs():
    s = mx_kscale(CV)
    t = mx_kscale(CF)
    tc, th = t[:CO], t[CO:]
    return {"context": bf(np.random.standard_normal((B, CV, H, W)) * 0.4 * s[None, :, None, None]),
            "high_feats": bf(np.random.standard_normal((B, CH, H, W)) * th[None, :, None, None]),
            "ww": bf(np.random.standard_normal((CO, CV)) * 2.0 / np.sqrt(CV) / s[None, :] * tc[:, None]),
            "bw": bf(np.random.standard_normal(CO) * 0.3 * tc),
            "wf": bf(np.random.standard_normal((CO, CF)) / np.sqrt(CF) / t[None, :]),
            "bfuse": bf(np.random.standard_normal(CO) * 0.3),
            "gf": bf(np.random.uniform(0.5, 1.5, CO)),
            "bef": bf(np.random.standard_normal(CO) * 0.3),
            "mf": bf(np.random.standard_normal(CO) * 0.3),
            "vf": bf(np.random.uniform(0.5, 1.5, CO))}


def reference(context, high_feats, ww, bw, wf, bfuse, gf, bef, mf, vf):
    ctx = f64(context).reshape(B, CV, N)
    hi = f64(high_feats).reshape(B, CH, N)
    c = (mxq(f64(ww), 1, "e4m3") @ mxq(ctx, 1, "e4m3")) + f64(bw)[None, :, None]
    fused = np.concatenate([c, hi], axis=1)
    y = (mxq(f64(wf), 1, "e4m3") @ mxq(fused, 1, "e4m3")) + f64(bfuse)[None, :, None]
    sc = f64(gf) / np.sqrt(f64(vf) + EPS)
    out = (y - f64(mf)[None, :, None]) * sc[None, :, None] + f64(bef)[None, :, None]
    return out.reshape(B, CO, H, W)

@@ -1,0 +1,246 @@
+from contextlib import ExitStack
+
+import concourse.mybir as mybir
+from concourse.masks import make_identity
+
+F32 = mybir.dt.float32
+BF16 = mybir.dt.bfloat16
+U32 = mybir.dt.uint32
+U8 = mybir.dt.uint8
+FP8X4 = mybir.dt.float8_e4m3fn_x4
+ACT = mybir.ActivationFunctionType
+ALU = mybir.AluOpType
+
+P = 128
+PACK = 4
+K_PASS = P * PACK
+WORDS_PASS = K_PASS // 2
+
+IMAGES = 2
+PIXELS = 24 * 24
+COLS = IMAGES * PIXELS
+C_CTX = 512
+C_MID = 1024
+C_HIGH = 2048
+C_FUSED = C_MID + C_HIGH
+C_OUT = 1024
+EPS = 1e-5
+
+MID_TILES = C_MID // P
+MID_PASSES = C_MID // K_PASS
+HIGH_PASSES = C_HIGH // K_PASS
+FUSED_PASSES = MID_PASSES + HIGH_PASSES
+OUT_TILES = C_OUT // P
+
+CHUNK = 512
+CHUNKS = ((0, 512), (512, 512), (1024, 128))
+PREPARE_NEXT_AT = 3
+
+FLOPS = 2 * COLS * (C_MID * C_CTX + C_OUT * C_FUSED)
+
+
+def image_pieces(col0, width):
+    pieces = []
+    for image in range(IMAGES):
+        lo = max(col0, image * PIXELS)
+        hi = min(col0 + width, (image + 1) * PIXELS)
+        if lo < hi:
+            pieces.append((image, lo - image * PIXELS, hi - lo, lo - col0))
+    return pieces
+
+
+def tile_afnb_pb_kernel(tc, context, high_feats, ww, bw, wf, bfuse, gf, bef, mf, vf, out):
+    nc = tc.nc
+    with ExitStack() as ctx:
+        keep = ctx.enter_context(tc.tile_pool(name="keep", bufs=1))
+        stage = ctx.enter_context(tc.tile_pool(name="stage", bufs=4))
+        flip_banks = ctx.enter_context(tc.psum_pool(name="flip_banks", bufs=4))
+        sum_banks = ctx.enter_context(tc.psum_pool(name="sum_banks", bufs=4))
+
+        identity = keep.tile([P, P], F32)
+        make_identity(nc, identity[:])
+
+        bw_bf = keep.tile([P, MID_TILES], BF16)
+        nc.scalar.dma_start(
+            out=bw_bf[:].rearrange("p (s e) -> p s e", e=2),
+            in_=bw.rearrange("(s p e) -> p s e", p=P, e=2),
+        )
+        per_channel = {}
+        for name, vector in (("bfuse", bfuse), ("gf", gf), ("bef", bef), ("mf", mf), ("vf", vf)):
+            per_channel[name] = keep.tile([P, OUT_TILES], BF16, name=name + "_bf")
+            nc.scalar.dma_start(out=per_channel[name][:], in_=vector.rearrange("(p m) -> p m", m=OUT_TILES))
+
+        def load_activations(rows, name):
+            raw = keep.tile([P, PACK, PIXELS], BF16, name=name)
+            nc.sync.dma_start(
+                out=raw[:].rearrange("p (u e) n -> p u e n", e=2),
+                in_=rows.rearrange("(u p e) h w -> p u e (h w)", p=P, e=2),
+            )
+            return raw
+
+        def load_high(image, g):
+            return load_activations(
+                high_feats[image, g * K_PASS : (g + 1) * K_PASS], "high_raw%d_%d" % (image, g)
+            )
+
+        wf_rows = wf.rearrange("(p m) k -> p m k", m=OUT_TILES)
+
+        def load_wf(m):
+            raw = keep.tile([P, C_FUSED], BF16, name="wf_raw%d" % m)
+            nc.sync.dma_start(out=raw[:], in_=wf_rows[:, m, :])
+            return raw
+
+        ww_raw = keep.tile([P, MID_TILES * C_CTX], BF16)
+        nc.sync.dma_start(
+            out=ww_raw[:].rearrange("p (s e k) -> p s e k", e=2, k=C_CTX),
+            in_=ww.rearrange("(s p e) k -> p s e k", p=P, e=2),
+        )
+        ctx_raw = [None] * IMAGES
+        high_raw = [[None] * HIGH_PASSES for image in range(IMAGES)]
+        wf_raw = [None] * OUT_TILES
+        ctx_raw[0] = load_activations(context[0], "ctx_raw0")
+        wf_raw[0] = load_wf(0)
+        for g in range(HIGH_PASSES):
+            high_raw[0][g] = load_high(0, g)
+        wf_raw[1] = load_wf(1)
+        wf_raw[2] = load_wf(2)
+        ctx_raw[1] = load_activations(context[1], "ctx_raw1")
+        for g in range(HIGH_PASSES):
+            wf_raw[3 + g] = load_wf(3 + g)
+            high_raw[1][g] = load_high(1, g)
+        wf_raw[7] = load_wf(7)
+
+        ww_codes = keep.tile([P, MID_TILES * P], U32, align_bytes=64)
+        ww_scales = keep.tile([P, MID_TILES * P], U8, align_bytes=64)
+        wf_codes = keep.tile([P, OUT_TILES * FUSED_PASSES * P], U32, align_bytes=64)
+        wf_scales = keep.tile([P, OUT_TILES * FUSED_PASSES * P], U8, align_bytes=64)
+        ctx_codes = keep.tile([P, COLS], U32, align_bytes=64)
+        ctx_scales = keep.tile([P, COLS], U8, align_bytes=64)
+        fused_codes = keep.tile([P, FUSED_PASSES, COLS], U32, align_bytes=64)
+        fused_scales = keep.tile([P, FUSED_PASSES, COLS], U8, align_bytes=64)
+
+        def quantise_weights(words, codes, scales):
+            flipped = flip_banks.tile([P, 4, P], F32)
+            for q in range(4):
+                nc.tensor.transpose(flipped[:, q, :], words[:, q * P : (q + 1) * P], identity[:])
+            grouped = stage.tile([P, 2 * P * PACK], BF16, name="w_grouped", align_bytes=64)
+            nc.scalar.copy(
+                out=grouped[:].bitcast(F32).rearrange("p (a r u) -> p a r u", a=2, u=2),
+                in_=flipped[:].rearrange("p (a u) r -> p a r u", u=2),
+            )
+            nc.vector.quantize_mx(out=codes.bitcast(FP8X4), scales=scales, in_=grouped[:])
+
+        def quantise_wf(m):
+            words = wf_raw[m][:].bitcast(F32)
+            for pair in range(FUSED_PASSES // 2):
+                cols = slice((m * FUSED_PASSES + 2 * pair) * P, (m * FUSED_PASSES + 2 * pair + 2) * P)
+                quantise_weights(
+                    words[:, 2 * pair * WORDS_PASS : (2 * pair + 2) * WORDS_PASS],
+                    wf_codes[:, cols],
+                    wf_scales[:, cols],
+                )
+
+        def quantise_columns(sources, width, codes, scales):
+            grouped = stage.tile([P, CHUNK, PACK], BF16, name="a_grouped", align_bytes=64)
+            for rows, first, number, offset in sources:
+                nc.vector.tensor_copy(
+                    out=grouped[:, offset : offset + number, :].rearrange("p (c i) t -> p c t i", i=4),
+                    in_=rows[:, :, first : first + number].rearrange("p t (c i) -> p c t i", i=4),
+                )
+            nc.vector.quantize_mx(
+                out=codes.bitcast(FP8X4),
+                scales=scales,
+                in_=grouped[:, :width, :].rearrange("p c t -> p (c t)"),
+            )
+
+        def prepare_activations(col0, width):
+            cols = slice(col0, col0 + width)
+            pieces = image_pieces(col0, width)
+            quantise_columns(
+                [(ctx_raw[image], first, number, offset) for image, first, number, offset in pieces],
+                width,
+                ctx_codes[:, cols],
+                ctx_scales[:, cols],
+            )
+            for g in range(HIGH_PASSES):
+                quantise_columns(
+                    [(high_raw[image][g], first, number, offset) for image, first, number, offset in pieces],
+                    width,
+                    fused_codes[:, MID_PASSES + g, cols],
+                    fused_scales[:, MID_PASSES + g, cols],
+                )
+            for g in range(MID_PASSES):
+                c_rows = stage.tile([P, PACK, CHUNK], BF16, name="c_rows", bufs=2)
+                for t in range(PACK):
+                    j = g * PACK + t
+                    c_sum = sum_banks.tile([P, CHUNK], F32, name="sums")
+                    nc.tensor.matmul_mx(
+                        out=c_sum[:, :width],
+                        lhsT=ww_codes[:, j * P : (j + 1) * P].bitcast(FP8X4),
+                        lhsT_scale=ww_scales[:, j * P : (j + 1) * P],
+                        rhs=ctx_codes[:, cols].bitcast(FP8X4),
+                        rhs_scale=ctx_scales[:, cols],
+                        start=True,
+                        stop=True,
+                    )
+                    nc.scalar.activation(
+                        out=c_rows[:, t, :width], in_=c_sum[:, :width], func=ACT.Identity,
+                        bias=bw_f32[:, j : j + 1], scale=1.0,
+                    )
+                quantise_columns(
+                    [(c_rows, 0, width, 0)], width, fused_codes[:, g, cols], fused_scales[:, g, cols]
+                )
+
+        def output_tile(m, col0, width):
+            cols = slice(col0, col0 + width)
+            y_sum = sum_banks.tile([P, CHUNK], F32, name="sums")
+            for g in range(FUSED_PASSES):
+                w_cols = slice((m * FUSED_PASSES + g) * P, (m * FUSED_PASSES + g + 1) * P)
+                nc.tensor.matmul_mx(
+                    out=y_sum[:, :width],
+                    lhsT=wf_codes[:, w_cols].bitcast(FP8X4),
+                    lhsT_scale=wf_scales[:, w_cols],
+                    rhs=fused_codes[:, g, cols].bitcast(FP8X4),
+                    rhs_scale=fused_scales[:, g, cols],
+                    start=(g == 0),
+                    stop=(g == FUSED_PASSES - 1),
+                )
+            result = stage.tile([P, CHUNK], F32, name="result")
+            nc.scalar.activation(
+                out=result[:, :width], in_=y_sum[:, :width], func=ACT.Identity,
+                bias=shift[:, m : m + 1], scale=gain[:, m : m + 1],
+            )
+            for image, first, number, offset in image_pieces(col0, width):
+                nc.sync.dma_start(
+                    out=out[image].rearrange("(p m) h w -> p m (h w)", m=OUT_TILES)[:, m, first : first + number],
+                    in_=result[:, offset : offset + number],
+                )
+
+        ww_words = ww_raw[:].bitcast(F32)
+        for pair in range(MID_TILES // 2):
+            quantise_weights(
+                ww_words[:, 2 * pair * WORDS_PASS : (2 * pair + 2) * WORDS_PASS],
+                ww_codes[:, 2 * pair * P : (2 * pair + 2) * P],
+                ww_scales[:, 2 * pair * P : (2 * pair + 2) * P],
+            )
+        bw_f32 = keep.tile([P, MID_TILES], F32)
+        nc.vector.tensor_copy(out=bw_f32[:], in_=bw_bf[:])
+        gain = keep.tile([P, OUT_TILES], F32)
+        shift = keep.tile([P, OUT_TILES], F32)
+        nc.vector.tensor_scalar_add(out=gain[:], in0=per_channel["vf"][:], scalar1=EPS)
+        nc.scalar.sqrt(out=gain[:], in_=gain[:])
+        nc.vector.reciprocal(out=gain[:], in_=gain[:])
+        nc.vector.tensor_mul(out=gain[:], in0=gain[:], in1=per_channel["gf"][:])
+        nc.vector.tensor_sub(out=shift[:], in0=per_channel["bfuse"][:], in1=per_channel["mf"][:])
+        nc.vector.tensor_mul(out=shift[:], in0=shift[:], in1=gain[:])
+        nc.vector.tensor_add(out=shift[:], in0=shift[:], in1=per_channel["bef"][:])
+
+        quantise_wf(0)
+        prepare_activations(*CHUNKS[0])
+        for index, (col0, width) in enumerate(CHUNKS):
+            for m in range(OUT_TILES):
+                if index == 0 and m + 1 < OUT_TILES:
+                    quantise_wf(m + 1)
+                if m == PREPARE_NEXT_AT and index + 1 < len(CHUNKS):
+                    prepare_activations(*CHUNKS[index + 1])
+                output_tile(m, col0, width)

@@ -9,7 +9,6 @@ U32 = mybir.dt.uint32
 U8 = mybir.dt.uint8
 FP8X4 = mybir.dt.float8_e4m3fn_x4
 ACT = mybir.ActivationFunctionType
-ALU = mybir.AluOpType
 
 P = 128
 PACK = 4
@@ -31,10 +30,14 @@ MID_PASSES = C_MID // K_PASS
 HIGH_PASSES = C_HIGH // K_PASS
 FUSED_PASSES = MID_PASSES + HIGH_PASSES
 OUT_TILES = C_OUT // P
+HALF = OUT_TILES // 2
 
 CHUNK = 512
 CHUNKS = ((0, 512), (512, 512), (1024, 128))
-PREPARE_NEXT_AT = 3
+WF_AHEAD = 2
+
+FIRST_BLOCK_STEP = 3
+FIRST_C_STEP = FIRST_BLOCK_STEP + 1
 
 FLOPS = 2 * COLS * (C_MID * C_CTX + C_OUT * C_FUSED)
 
@@ -52,10 +55,11 @@ def image_pieces(col0, width):
 def tile_afnb_pb_kernel(tc, context, high_feats, ww, bw, wf, bfuse, gf, bef, mf, vf, out):
     nc = tc.nc
     with ExitStack() as ctx:
+        ctx.enter_context(tc.manual_schedule())
         keep = ctx.enter_context(tc.tile_pool(name="keep", bufs=1))
         stage = ctx.enter_context(tc.tile_pool(name="stage", bufs=4))
-        flip_banks = ctx.enter_context(tc.psum_pool(name="flip_banks", bufs=4))
-        sum_banks = ctx.enter_context(tc.psum_pool(name="sum_banks", bufs=4))
+        short_banks = ctx.enter_context(tc.psum_pool(name="short_banks", bufs=4))
+        sum_banks = ctx.enter_context(tc.psum_pool(name="sum_banks", bufs=HALF))
 
         identity = keep.tile([P, P], F32)
         make_identity(nc, identity[:])
@@ -66,7 +70,7 @@ def tile_afnb_pb_kernel(tc, context, high_feats, ww, bw, wf, bfuse, gf, bef, mf,
             in_=bw.rearrange("(s p e) -> p s e", p=P, e=2),
         )
         per_channel = {}
-        for name, vector in (("bfuse", bfuse), ("gf", gf), ("bef", bef), ("mf", mf), ("vf", vf)):
+        for name, vector in (("vf", vf), ("gf", gf), ("bfuse", bfuse), ("mf", mf), ("bef", bef)):
             per_channel[name] = keep.tile([P, OUT_TILES], BF16, name=name + "_bf")
             nc.scalar.dma_start(out=per_channel[name][:], in_=vector.rearrange("(p m) -> p m", m=OUT_TILES))
 
@@ -78,37 +82,42 @@ def tile_afnb_pb_kernel(tc, context, high_feats, ww, bw, wf, bfuse, gf, bef, mf,
             )
             return raw
 
-        def load_high(image, g):
-            return load_activations(
-                high_feats[image, g * K_PASS : (g + 1) * K_PASS], "high_raw%d_%d" % (image, g)
+        ctx_raw = [None] * IMAGES
+        high_raw = [[None] * HIGH_PASSES for image in range(IMAGES)]
+        wf_raw = [None] * OUT_TILES
+
+        def load_context(image):
+            ctx_raw[image] = load_activations(context[image], "ctx_raw%d" % image)
+
+        def load_high(image, h):
+            high_raw[image][h] = load_activations(
+                high_feats[image, h * K_PASS : (h + 1) * K_PASS], "high_raw%d_%d" % (image, h)
             )
 
-        wf_rows = wf.rearrange("(p m) k -> p m k", m=OUT_TILES)
-
         def load_wf(m):
-            raw = keep.tile([P, C_FUSED], BF16, name="wf_raw%d" % m)
-            nc.sync.dma_start(out=raw[:], in_=wf_rows[:, m, :])
-            return raw
+            wf_raw[m] = keep.tile([P, C_FUSED], BF16, name="wf_raw%d" % m)
+            nc.sync.dma_start(out=wf_raw[m][:], in_=wf.rearrange("(p m) k -> p m k", m=OUT_TILES)[:, m, :])
 
+        load_context(0)
+        load_high(0, 0)
         ww_raw = keep.tile([P, MID_TILES * C_CTX], BF16)
         nc.sync.dma_start(
             out=ww_raw[:].rearrange("p (s e k) -> p s e k", e=2, k=C_CTX),
             in_=ww.rearrange("(s p e) k -> p s e k", p=P, e=2),
         )
-        ctx_raw = [None] * IMAGES
-        high_raw = [[None] * HIGH_PASSES for image in range(IMAGES)]
-        wf_raw = [None] * OUT_TILES
-        ctx_raw[0] = load_activations(context[0], "ctx_raw0")
-        wf_raw[0] = load_wf(0)
-        for g in range(HIGH_PASSES):
-            high_raw[0][g] = load_high(0, g)
-        wf_raw[1] = load_wf(1)
-        wf_raw[2] = load_wf(2)
-        ctx_raw[1] = load_activations(context[1], "ctx_raw1")
-        for g in range(HIGH_PASSES):
-            wf_raw[3 + g] = load_wf(3 + g)
-            high_raw[1][g] = load_high(1, g)
-        wf_raw[7] = load_wf(7)
+        load_high(0, 1)
+        load_high(0, 2)
+        load_wf(0)
+        load_high(0, 3)
+        for m in range(1, HALF + WF_AHEAD):
+            load_wf(m)
+        load_context(1)
+        load_high(1, 0)
+        load_wf(6)
+        load_high(1, 1)
+        load_wf(7)
+        load_high(1, 2)
+        load_high(1, 3)
 
         ww_codes = keep.tile([P, MID_TILES * P], U32, align_bytes=64)
         ww_scales = keep.tile([P, MID_TILES * P], U8, align_bytes=64)
@@ -119,82 +128,94 @@ def tile_afnb_pb_kernel(tc, context, high_feats, ww, bw, wf, bfuse, gf, bef, mf,
         fused_codes = keep.tile([P, FUSED_PASSES, COLS], U32, align_bytes=64)
         fused_scales = keep.tile([P, FUSED_PASSES, COLS], U8, align_bytes=64)
 
-        def quantise_weights(words, codes, scales):
-            flipped = flip_banks.tile([P, 4, P], F32)
-            for q in range(4):
-                nc.tensor.transpose(flipped[:, q, :], words[:, q * P : (q + 1) * P], identity[:])
-            grouped = stage.tile([P, 2 * P * PACK], BF16, name="w_grouped", align_bytes=64)
-            nc.scalar.copy(
-                out=grouped[:].bitcast(F32).rearrange("p (a r u) -> p a r u", a=2, u=2),
-                in_=flipped[:].rearrange("p (a u) r -> p a r u", u=2),
-            )
-            nc.vector.quantize_mx(out=codes.bitcast(FP8X4), scales=scales, in_=grouped[:])
+        def transpose_weights(raw, pairs):
+            words = raw[:].bitcast(F32)
+            grouped_pairs = []
+            for pair in range(pairs):
+                flipped = short_banks.tile([P, 4, P], F32, name="short")
+                for q in range(4):
+                    first = (4 * pair + q) * P
+                    nc.tensor.transpose(flipped[:, q, :], words[:, first : first + P], identity[:])
+                grouped = stage.tile([P, 2 * P * PACK], BF16, name="w_grouped", bufs=6, align_bytes=64)
+                nc.scalar.copy(
+                    out=grouped[:].bitcast(F32).rearrange("p (a r u) -> p a r u", a=2, u=2),
+                    in_=flipped[:].rearrange("p (a u) r -> p a r u", u=2),
+                )
+                grouped_pairs.append(grouped)
+            return grouped_pairs
+
+        def quantise_weights(grouped_pairs, codes, scales, first_operand):
+            for pair, grouped in enumerate(grouped_pairs):
+                cols = slice((first_operand + 2 * pair) * P, (first_operand + 2 * pair + 2) * P)
+                nc.vector.quantize_mx(out=codes[:, cols].bitcast(FP8X4), scales=scales[:, cols], in_=grouped[:])
+
+        wf_grouped = [None] * OUT_TILES
+
+        def transpose_wf(m):
+            wf_grouped[m] = transpose_weights(wf_raw[m], FUSED_PASSES // 2)
 
         def quantise_wf(m):
-            words = wf_raw[m][:].bitcast(F32)
-            for pair in range(FUSED_PASSES // 2):
-                cols = slice((m * FUSED_PASSES + 2 * pair) * P, (m * FUSED_PASSES + 2 * pair + 2) * P)
-                quantise_weights(
-                    words[:, 2 * pair * WORDS_PASS : (2 * pair + 2) * WORDS_PASS],
-                    wf_codes[:, cols],
-                    wf_scales[:, cols],
-                )
+            quantise_weights(wf_grouped[m], wf_codes, wf_scales, m * FUSED_PASSES)
 
-        def quantise_columns(sources, width, codes, scales):
+        def regroup(sources):
             grouped = stage.tile([P, CHUNK, PACK], BF16, name="a_grouped", align_bytes=64)
             for rows, first, number, offset in sources:
                 nc.vector.tensor_copy(
                     out=grouped[:, offset : offset + number, :].rearrange("p (c i) t -> p c t i", i=4),
                     in_=rows[:, :, first : first + number].rearrange("p t (c i) -> p c t i", i=4),
                 )
+            return grouped
+
+        def quantise(grouped, width, codes, scales):
             nc.vector.quantize_mx(
                 out=codes.bitcast(FP8X4),
                 scales=scales,
                 in_=grouped[:, :width, :].rearrange("p c t -> p (c t)"),
             )
 
-        def prepare_activations(col0, width):
-            cols = slice(col0, col0 + width)
-            pieces = image_pieces(col0, width)
-            quantise_columns(
-                [(ctx_raw[image], first, number, offset) for image, first, number, offset in pieces],
-                width,
-                ctx_codes[:, cols],
-                ctx_scales[:, cols],
-            )
-            for g in range(HIGH_PASSES):
-                quantise_columns(
-                    [(high_raw[image][g], first, number, offset) for image, first, number, offset in pieces],
-                    width,
-                    fused_codes[:, MID_PASSES + g, cols],
-                    fused_scales[:, MID_PASSES + g, cols],
-                )
-            for g in range(MID_PASSES):
-                c_rows = stage.tile([P, PACK, CHUNK], BF16, name="c_rows", bufs=2)
-                for t in range(PACK):
-                    j = g * PACK + t
-                    c_sum = sum_banks.tile([P, CHUNK], F32, name="sums")
-                    nc.tensor.matmul_mx(
-                        out=c_sum[:, :width],
-                        lhsT=ww_codes[:, j * P : (j + 1) * P].bitcast(FP8X4),
-                        lhsT_scale=ww_scales[:, j * P : (j + 1) * P],
-                        rhs=ctx_codes[:, cols].bitcast(FP8X4),
-                        rhs_scale=ctx_scales[:, cols],
-                        start=True,
-                        stop=True,
-                    )
-                    nc.scalar.activation(
-                        out=c_rows[:, t, :width], in_=c_sum[:, :width], func=ACT.Identity,
-                        bias=bw_f32[:, j : j + 1], scale=1.0,
-                    )
-                quantise_columns(
-                    [(c_rows, 0, width, 0)], width, fused_codes[:, g, cols], fused_scales[:, g, cols]
-                )
+        c_rows = [None] * MID_PASSES
 
-        def output_tile(m, col0, width):
+        def regroup_block(block, col0, width):
+            pieces = image_pieces(col0, width)
+            if block == 0:
+                return regroup([(ctx_raw[image], first, number, offset) for image, first, number, offset in pieces])
+            if block <= HIGH_PASSES:
+                return regroup(
+                    [(high_raw[image][block - 1], first, number, offset) for image, first, number, offset in pieces]
+                )
+            return regroup([(c_rows[block - 1 - HIGH_PASSES], 0, width, 0)])
+
+        def quantise_block(block, grouped, col0, width):
             cols = slice(col0, col0 + width)
-            y_sum = sum_banks.tile([P, CHUNK], F32, name="sums")
-            for g in range(FUSED_PASSES):
+            if block == 0:
+                quantise(grouped, width, ctx_codes[:, cols], ctx_scales[:, cols])
+            else:
+                g = MID_PASSES + block - 1 if block <= HIGH_PASSES else block - 1 - HIGH_PASSES
+                quantise(grouped, width, fused_codes[:, g, cols], fused_scales[:, g, cols])
+
+        def c_tile(j, col0, width):
+            cols = slice(col0, col0 + width)
+            g, t = divmod(j, PACK)
+            if t == 0:
+                c_rows[g] = stage.tile([P, PACK, CHUNK], BF16, name="c_rows", bufs=MID_PASSES)
+            c_sum = short_banks.tile([P, CHUNK], F32, name="short")
+            nc.tensor.matmul_mx(
+                out=c_sum[:, :width],
+                lhsT=ww_codes[:, j * P : (j + 1) * P].bitcast(FP8X4),
+                lhsT_scale=ww_scales[:, j * P : (j + 1) * P],
+                rhs=ctx_codes[:, cols].bitcast(FP8X4),
+                rhs_scale=ctx_scales[:, cols],
+                start=True,
+                stop=True,
+            )
+            nc.scalar.activation(
+                out=c_rows[g][:, t, :width], in_=c_sum[:, :width], func=ACT.Identity,
+                bias=bw_f32[:, j : j + 1], scale=1.0,
+            )
+
+        def y_passes(y_sum, m, passes, col0, width):
+            cols = slice(col0, col0 + width)
+            for g in passes:
                 w_cols = slice((m * FUSED_PASSES + g) * P, (m * FUSED_PASSES + g + 1) * P)
                 nc.tensor.matmul_mx(
                     out=y_sum[:, :width],
@@ -202,9 +223,11 @@ def tile_afnb_pb_kernel(tc, context, high_feats, ww, bw, wf, bfuse, gf, bef, mf,
                     lhsT_scale=wf_scales[:, w_cols],
                     rhs=fused_codes[:, g, cols].bitcast(FP8X4),
                     rhs_scale=fused_scales[:, g, cols],
-                    start=(g == 0),
-                    stop=(g == FUSED_PASSES - 1),
+                    start=(g == MID_PASSES),
+                    stop=(g == MID_PASSES - 1),
                 )
+
+        def finish_tile(y_sum, m, col0, width):
             result = stage.tile([P, CHUNK], F32, name="result")
             nc.scalar.activation(
                 out=result[:, :width], in_=y_sum[:, :width], func=ACT.Identity,
@@ -216,31 +239,64 @@ def tile_afnb_pb_kernel(tc, context, high_feats, ww, bw, wf, bfuse, gf, bef, mf,
                     in_=result[:, offset : offset + number],
                 )
 
-        ww_words = ww_raw[:].bitcast(F32)
-        for pair in range(MID_TILES // 2):
-            quantise_weights(
-                ww_words[:, 2 * pair * WORDS_PASS : (2 * pair + 2) * WORDS_PASS],
-                ww_codes[:, 2 * pair * P : (2 * pair + 2) * P],
-                ww_scales[:, 2 * pair * P : (2 * pair + 2) * P],
-            )
+        first_chunk = CHUNKS[0]
         bw_f32 = keep.tile([P, MID_TILES], F32)
-        nc.vector.tensor_copy(out=bw_f32[:], in_=bw_bf[:])
         gain = keep.tile([P, OUT_TILES], F32)
         shift = keep.tile([P, OUT_TILES], F32)
         nc.vector.tensor_scalar_add(out=gain[:], in0=per_channel["vf"][:], scalar1=EPS)
         nc.scalar.sqrt(out=gain[:], in_=gain[:])
+        nc.vector.tensor_copy(out=bw_f32[:], in_=bw_bf[:])
+
+        for block in (0, 1):
+            quantise_block(block, regroup_block(block, *first_chunk), *first_chunk)
         nc.vector.reciprocal(out=gain[:], in_=gain[:])
         nc.vector.tensor_mul(out=gain[:], in0=gain[:], in1=per_channel["gf"][:])
         nc.vector.tensor_sub(out=shift[:], in0=per_channel["bfuse"][:], in1=per_channel["mf"][:])
         nc.vector.tensor_mul(out=shift[:], in0=shift[:], in1=gain[:])
         nc.vector.tensor_add(out=shift[:], in0=shift[:], in1=per_channel["bef"][:])
 
+        quantise_weights(transpose_weights(ww_raw, MID_TILES // 2), ww_codes, ww_scales, 0)
+        for j in range(PACK):
+            c_tile(j, *first_chunk)
+        grouped_2 = regroup_block(2, *first_chunk)
+        grouped_3 = regroup_block(3, *first_chunk)
+        quantise_block(2, grouped_2, *first_chunk)
+        quantise_block(3, grouped_3, *first_chunk)
+        transpose_wf(0)
+        for j in range(PACK, MID_TILES):
+            c_tile(j, *first_chunk)
+        grouped_4 = regroup_block(4, *first_chunk)
         quantise_wf(0)
-        prepare_activations(*CHUNKS[0])
+        quantise_block(4, grouped_4, *first_chunk)
+        transpose_wf(1)
+        grouped_5 = regroup_block(5, *first_chunk)
+        grouped_6 = regroup_block(6, *first_chunk)
+        quantise_block(5, grouped_5, *first_chunk)
+        quantise_block(6, grouped_6, *first_chunk)
+
+        def prepare_next(index, step):
+            if index + 1 == len(CHUNKS):
+                return
+            following = CHUNKS[index + 1]
+            if 0 <= step - FIRST_C_STEP < MID_TILES:
+                c_tile(step - FIRST_C_STEP, *following)
+            if step >= FIRST_BLOCK_STEP and (step - FIRST_BLOCK_STEP) % 2 == 0:
+                block = (step - FIRST_BLOCK_STEP) // 2
+                quantise_block(block, regroup_block(block, *following), *following)
+
         for index, (col0, width) in enumerate(CHUNKS):
-            for m in range(OUT_TILES):
-                if index == 0 and m + 1 < OUT_TILES:
-                    quantise_wf(m + 1)
-                if m == PREPARE_NEXT_AT and index + 1 < len(CHUNKS):
-                    prepare_activations(*CHUNKS[index + 1])
-                output_tile(m, col0, width)
+            for half in range(2):
+                tiles = range(half * HALF, (half + 1) * HALF)
+                y_sums = {}
+                for m in tiles:
+                    if index == 0 and m + 1 < OUT_TILES:
+                        quantise_wf(m + 1)
+                    prepare_next(index, 2 * half * HALF + m % HALF)
+                    y_sums[m] = sum_banks.tile([P, CHUNK], F32, name="y_sum")
+                    y_passes(y_sums[m], m, range(MID_PASSES, FUSED_PASSES), col0, width)
+                    if index == 0 and m + WF_AHEAD < OUT_TILES:
+                        transpose_wf(m + WF_AHEAD)
+                for m in tiles:
+                    prepare_next(index, (2 * half + 1) * HALF + m % HALF)
+                    y_passes(y_sums[m], m, range(MID_PASSES), col0, width)
+                    finish_tile(y_sums[m], m, col0, width)

@@ -36,8 +36,11 @@ CHUNK = 512
 CHUNKS = ((0, 512), (512, 512), (1024, 128))
 WF_AHEAD = 2
 
-FIRST_BLOCK_STEP = 3
+STEPS = 4 * HALF
+FIRST_BLOCK_STEP = STEPS // 2
+BLOCKS = 1 + HIGH_PASSES + MID_PASSES
 FIRST_C_STEP = FIRST_BLOCK_STEP + 1
+C_TILES_A_STEP = 2
 
 FLOPS = 2 * COLS * (C_MID * C_CTX + C_OUT * C_FUSED)
 
@@ -109,15 +112,11 @@ def tile_afnb_pb_kernel(tc, context, high_feats, ww, bw, wf, bfuse, gf, bef, mf,
         load_high(0, 2)
         load_wf(0)
         load_high(0, 3)
-        for m in range(1, HALF + WF_AHEAD):
+        for m in range(1, OUT_TILES):
             load_wf(m)
         load_context(1)
-        load_high(1, 0)
-        load_wf(6)
-        load_high(1, 1)
-        load_wf(7)
-        load_high(1, 2)
-        load_high(1, 3)
+        for h in range(HIGH_PASSES):
+            load_high(1, h)
 
         ww_codes = keep.tile([P, MID_TILES * P], U32, align_bytes=64)
         ww_scales = keep.tile([P, MID_TILES * P], U8, align_bytes=64)
@@ -228,7 +227,9 @@ def tile_afnb_pb_kernel(tc, context, high_feats, ww, bw, wf, bfuse, gf, bef, mf,
                 )
 
         def finish_tile(y_sum, m, col0, width):
-            result = stage.tile([P, CHUNK], F32, name="result")
+            result = stage.tile(
+                [P, width], F32, name="result%d" % width, bufs=(HALF if width == CHUNK else OUT_TILES)
+            )
             nc.scalar.activation(
                 out=result[:, :width], in_=y_sum[:, :width], func=ACT.Identity,
                 bias=shift[:, m : m + 1], scale=gain[:, m : m + 1],
@@ -270,18 +271,19 @@ def tile_afnb_pb_kernel(tc, context, high_feats, ww, bw, wf, bfuse, gf, bef, mf,
         quantise_block(4, grouped_4, *first_chunk)
         transpose_wf(1)
         grouped_5 = regroup_block(5, *first_chunk)
-        grouped_6 = regroup_block(6, *first_chunk)
+        quantise_wf(1)
         quantise_block(5, grouped_5, *first_chunk)
-        quantise_block(6, grouped_6, *first_chunk)
+        quantise_block(6, regroup_block(6, *first_chunk), *first_chunk)
 
         def prepare_next(index, step):
             if index + 1 == len(CHUNKS):
                 return
             following = CHUNKS[index + 1]
-            if 0 <= step - FIRST_C_STEP < MID_TILES:
-                c_tile(step - FIRST_C_STEP, *following)
-            if step >= FIRST_BLOCK_STEP and (step - FIRST_BLOCK_STEP) % 2 == 0:
-                block = (step - FIRST_BLOCK_STEP) // 2
+            for j in range(C_TILES_A_STEP * (step - FIRST_C_STEP), C_TILES_A_STEP * (step - FIRST_C_STEP + 1)):
+                if 0 <= j < MID_TILES:
+                    c_tile(j, *following)
+            block = step - FIRST_BLOCK_STEP
+            if 0 <= block < BLOCKS:
                 quantise_block(block, regroup_block(block, *following), *following)
 
         for index, (col0, width) in enumerate(CHUNKS):
@@ -289,13 +291,12 @@ def tile_afnb_pb_kernel(tc, context, high_feats, ww, bw, wf, bfuse, gf, bef, mf,
                 tiles = range(half * HALF, (half + 1) * HALF)
                 y_sums = {}
                 for m in tiles:
-                    if index == 0 and m + 1 < OUT_TILES:
-                        quantise_wf(m + 1)
                     prepare_next(index, 2 * half * HALF + m % HALF)
                     y_sums[m] = sum_banks.tile([P, CHUNK], F32, name="y_sum")
                     y_passes(y_sums[m], m, range(MID_PASSES, FUSED_PASSES), col0, width)
                     if index == 0 and m + WF_AHEAD < OUT_TILES:
                         transpose_wf(m + WF_AHEAD)
+                        quantise_wf(m + WF_AHEAD)
                 for m in tiles:
                     prepare_next(index, (2 * half + 1) * HALF + m % HALF)
                     y_passes(y_sums[m], m, range(MID_PASSES), col0, width)

@@ -58,7 +58,6 @@ def image_pieces(col0, width):
 def tile_afnb_pb_kernel(tc, context, high_feats, ww, bw, wf, bfuse, gf, bef, mf, vf, out):
     nc = tc.nc
     with ExitStack() as ctx:
-        ctx.enter_context(tc.manual_schedule())
         keep = ctx.enter_context(tc.tile_pool(name="keep", bufs=1))
         stage = ctx.enter_context(tc.tile_pool(name="stage", bufs=4))
         short_banks = ctx.enter_context(tc.psum_pool(name="short_banks", bufs=4))

@@ -227,7 +227,7 @@ def tile_afnb_pb_kernel(tc, context, high_feats, ww, bw, wf, bfuse, gf, bef, mf,
 
         def finish_tile(y_sum, m, col0, width):
             result = stage.tile(
-                [P, width], F32, name="result%d" % width, bufs=(HALF if width == CHUNK else OUT_TILES)
+                [P, width], F32, name="result%d" % width, bufs=HALF
             )
             nc.scalar.activation(
                 out=result[:, :width], in_=y_sum[:, :width], func=ACT.Identity,

from contextlib import ExitStack

import concourse.mybir as mybir
from concourse.masks import make_identity

F32 = mybir.dt.float32
BF16 = mybir.dt.bfloat16
U32 = mybir.dt.uint32
U8 = mybir.dt.uint8
FP8X4 = mybir.dt.float8_e4m3fn_x4
ACT = mybir.ActivationFunctionType

P = 128
PACK = 4
K_PASS = P * PACK
WORDS_PASS = K_PASS // 2

IMAGES = 2
PIXELS = 24 * 24
COLS = IMAGES * PIXELS
C_CTX = 512
C_MID = 1024
C_HIGH = 2048
C_FUSED = C_MID + C_HIGH
C_OUT = 1024
EPS = 1e-5

MID_TILES = C_MID // P
MID_PASSES = C_MID // K_PASS
HIGH_PASSES = C_HIGH // K_PASS
FUSED_PASSES = MID_PASSES + HIGH_PASSES
OUT_TILES = C_OUT // P
HALF = OUT_TILES // 2

CHUNK = 512
CHUNKS = ((0, 512), (512, 512), (1024, 128))
WF_AHEAD = 2

STEPS = 4 * HALF
FIRST_BLOCK_STEP = STEPS // 2
BLOCKS = 1 + HIGH_PASSES + MID_PASSES
FIRST_C_STEP = FIRST_BLOCK_STEP + 1
C_TILES_A_STEP = 2

FLOPS = 2 * COLS * (C_MID * C_CTX + C_OUT * C_FUSED)


def image_pieces(col0, width):
    pieces = []
    for image in range(IMAGES):
        lo = max(col0, image * PIXELS)
        hi = min(col0 + width, (image + 1) * PIXELS)
        if lo < hi:
            pieces.append((image, lo - image * PIXELS, hi - lo, lo - col0))
    return pieces


def tile_afnb_pb_kernel(tc, context, high_feats, ww, bw, wf, bfuse, gf, bef, mf, vf, out):
    nc = tc.nc
    with ExitStack() as ctx:
        keep = ctx.enter_context(tc.tile_pool(name="keep", bufs=1))
        stage = ctx.enter_context(tc.tile_pool(name="stage", bufs=4))
        short_banks = ctx.enter_context(tc.psum_pool(name="short_banks", bufs=4))
        sum_banks = ctx.enter_context(tc.psum_pool(name="sum_banks", bufs=HALF))

        identity = keep.tile([P, P], F32)
        make_identity(nc, identity[:])

        bw_bf = keep.tile([P, MID_TILES], BF16)
        nc.scalar.dma_start(
            out=bw_bf[:].rearrange("p (s e) -> p s e", e=2),
            in_=bw.rearrange("(s p e) -> p s e", p=P, e=2),
        )
        per_channel = {}
        for name, vector in (("vf", vf), ("gf", gf), ("bfuse", bfuse), ("mf", mf), ("bef", bef)):
            per_channel[name] = keep.tile([P, OUT_TILES], BF16, name=name + "_bf")
            nc.scalar.dma_start(out=per_channel[name][:], in_=vector.rearrange("(p m) -> p m", m=OUT_TILES))

        def load_activations(rows, name):
            raw = keep.tile([P, PACK, PIXELS], BF16, name=name)
            nc.sync.dma_start(
                out=raw[:].rearrange("p (u e) n -> p u e n", e=2),
                in_=rows.rearrange("(u p e) h w -> p u e (h w)", p=P, e=2),
            )
            return raw

        ctx_raw = [None] * IMAGES
        high_raw = [[None] * HIGH_PASSES for image in range(IMAGES)]
        wf_raw = [None] * OUT_TILES

        def load_context(image):
            ctx_raw[image] = load_activations(context[image], "ctx_raw%d" % image)

        def load_high(image, h):
            high_raw[image][h] = load_activations(
                high_feats[image, h * K_PASS : (h + 1) * K_PASS], "high_raw%d_%d" % (image, h)
            )

        def load_wf(m):
            wf_raw[m] = keep.tile([P, C_FUSED], BF16, name="wf_raw%d" % m)
            nc.sync.dma_start(out=wf_raw[m][:], in_=wf.rearrange("(p m) k -> p m k", m=OUT_TILES)[:, m, :])

        load_context(0)
        load_high(0, 0)
        ww_raw = keep.tile([P, MID_TILES * C_CTX], BF16)
        nc.sync.dma_start(
            out=ww_raw[:].rearrange("p (s e k) -> p s e k", e=2, k=C_CTX),
            in_=ww.rearrange("(s p e) k -> p s e k", p=P, e=2),
        )
        load_high(0, 1)
        load_high(0, 2)
        load_wf(0)
        load_high(0, 3)
        for m in range(1, OUT_TILES):
            load_wf(m)
        load_context(1)
        for h in range(HIGH_PASSES):
            load_high(1, h)

        ww_codes = keep.tile([P, MID_TILES * P], U32, align_bytes=64)
        ww_scales = keep.tile([P, MID_TILES * P], U8, align_bytes=64)
        wf_codes = keep.tile([P, OUT_TILES * FUSED_PASSES * P], U32, align_bytes=64)
        wf_scales = keep.tile([P, OUT_TILES * FUSED_PASSES * P], U8, align_bytes=64)
        ctx_codes = keep.tile([P, COLS], U32, align_bytes=64)
        ctx_scales = keep.tile([P, COLS], U8, align_bytes=64)
        fused_codes = keep.tile([P, FUSED_PASSES, COLS], U32, align_bytes=64)
        fused_scales = keep.tile([P, FUSED_PASSES, COLS], U8, align_bytes=64)

        def transpose_weights(raw, pairs):
            words = raw[:].bitcast(F32)
            grouped_pairs = []
            for pair in range(pairs):
                flipped = short_banks.tile([P, 4, P], F32, name="short")
                for q in range(4):
                    first = (4 * pair + q) * P
                    nc.tensor.transpose(flipped[:, q, :], words[:, first : first + P], identity[:])
                grouped = stage.tile([P, 2 * P * PACK], BF16, name="w_grouped", bufs=6, align_bytes=64)
                nc.scalar.copy(
                    out=grouped[:].bitcast(F32).rearrange("p (a r u) -> p a r u", a=2, u=2),
                    in_=flipped[:].rearrange("p (a u) r -> p a r u", u=2),
                )
                grouped_pairs.append(grouped)
            return grouped_pairs

        def quantise_weights(grouped_pairs, codes, scales, first_operand):
            for pair, grouped in enumerate(grouped_pairs):
                cols = slice((first_operand + 2 * pair) * P, (first_operand + 2 * pair + 2) * P)
                nc.vector.quantize_mx(out=codes[:, cols].bitcast(FP8X4), scales=scales[:, cols], in_=grouped[:])

        wf_grouped = [None] * OUT_TILES

        def transpose_wf(m):
            wf_grouped[m] = transpose_weights(wf_raw[m], FUSED_PASSES // 2)

        def quantise_wf(m):
            quantise_weights(wf_grouped[m], wf_codes, wf_scales, m * FUSED_PASSES)

        def regroup(sources):
            grouped = stage.tile([P, CHUNK, PACK], BF16, name="a_grouped", align_bytes=64)
            for rows, first, number, offset in sources:
                nc.vector.tensor_copy(
                    out=grouped[:, offset : offset + number, :].rearrange("p (c i) t -> p c t i", i=4),
                    in_=rows[:, :, first : first + number].rearrange("p t (c i) -> p c t i", i=4),
                )
            return grouped

        def quantise(grouped, width, codes, scales):
            nc.vector.quantize_mx(
                out=codes.bitcast(FP8X4),
                scales=scales,
                in_=grouped[:, :width, :].rearrange("p c t -> p (c t)"),
            )

        c_rows = [None] * MID_PASSES

        def regroup_block(block, col0, width):
            pieces = image_pieces(col0, width)
            if block == 0:
                return regroup([(ctx_raw[image], first, number, offset) for image, first, number, offset in pieces])
            if block <= HIGH_PASSES:
                return regroup(
                    [(high_raw[image][block - 1], first, number, offset) for image, first, number, offset in pieces]
                )
            return regroup([(c_rows[block - 1 - HIGH_PASSES], 0, width, 0)])

        def quantise_block(block, grouped, col0, width):
            cols = slice(col0, col0 + width)
            if block == 0:
                quantise(grouped, width, ctx_codes[:, cols], ctx_scales[:, cols])
            else:
                g = MID_PASSES + block - 1 if block <= HIGH_PASSES else block - 1 - HIGH_PASSES
                quantise(grouped, width, fused_codes[:, g, cols], fused_scales[:, g, cols])

        def c_tile(j, col0, width):
            cols = slice(col0, col0 + width)
            g, t = divmod(j, PACK)
            if t == 0:
                c_rows[g] = stage.tile([P, PACK, CHUNK], BF16, name="c_rows", bufs=MID_PASSES)
            c_sum = short_banks.tile([P, CHUNK], F32, name="short")
            nc.tensor.matmul_mx(
                out=c_sum[:, :width],
                lhsT=ww_codes[:, j * P : (j + 1) * P].bitcast(FP8X4),
                lhsT_scale=ww_scales[:, j * P : (j + 1) * P],
                rhs=ctx_codes[:, cols].bitcast(FP8X4),
                rhs_scale=ctx_scales[:, cols],
                start=True,
                stop=True,
            )
            nc.scalar.activation(
                out=c_rows[g][:, t, :width], in_=c_sum[:, :width], func=ACT.Identity,
                bias=bw_f32[:, j : j + 1], scale=1.0,
            )

        def y_passes(y_sum, m, passes, col0, width):
            cols = slice(col0, col0 + width)
            for g in passes:
                w_cols = slice((m * FUSED_PASSES + g) * P, (m * FUSED_PASSES + g + 1) * P)
                nc.tensor.matmul_mx(
                    out=y_sum[:, :width],
                    lhsT=wf_codes[:, w_cols].bitcast(FP8X4),
                    lhsT_scale=wf_scales[:, w_cols],
                    rhs=fused_codes[:, g, cols].bitcast(FP8X4),
                    rhs_scale=fused_scales[:, g, cols],
                    start=(g == MID_PASSES),
                    stop=(g == MID_PASSES - 1),
                )

        def finish_tile(y_sum, m, col0, width):
            result = stage.tile(
                [P, width], F32, name="result%d" % width, bufs=HALF
            )
            nc.scalar.activation(
                out=result[:, :width], in_=y_sum[:, :width], func=ACT.Identity,
                bias=shift[:, m : m + 1], scale=gain[:, m : m + 1],
            )
            for image, first, number, offset in image_pieces(col0, width):
                nc.sync.dma_start(
                    out=out[image].rearrange("(p m) h w -> p m (h w)", m=OUT_TILES)[:, m, first : first + number],
                    in_=result[:, offset : offset + number],
                )

        first_chunk = CHUNKS[0]
        bw_f32 = keep.tile([P, MID_TILES], F32)
        gain = keep.tile([P, OUT_TILES], F32)
        shift = keep.tile([P, OUT_TILES], F32)
        nc.vector.tensor_scalar_add(out=gain[:], in0=per_channel["vf"][:], scalar1=EPS)
        nc.scalar.sqrt(out=gain[:], in_=gain[:])
        nc.vector.tensor_copy(out=bw_f32[:], in_=bw_bf[:])

        for block in (0, 1):
            quantise_block(block, regroup_block(block, *first_chunk), *first_chunk)
        nc.vector.reciprocal(out=gain[:], in_=gain[:])
        nc.vector.tensor_mul(out=gain[:], in0=gain[:], in1=per_channel["gf"][:])
        nc.vector.tensor_sub(out=shift[:], in0=per_channel["bfuse"][:], in1=per_channel["mf"][:])
        nc.vector.tensor_mul(out=shift[:], in0=shift[:], in1=gain[:])
        nc.vector.tensor_add(out=shift[:], in0=shift[:], in1=per_channel["bef"][:])

        quantise_weights(transpose_weights(ww_raw, MID_TILES // 2), ww_codes, ww_scales, 0)
        for j in range(PACK):
            c_tile(j, *first_chunk)
        grouped_2 = regroup_block(2, *first_chunk)
        grouped_3 = regroup_block(3, *first_chunk)
        quantise_block(2, grouped_2, *first_chunk)
        quantise_block(3, grouped_3, *first_chunk)
        transpose_wf(0)
        for j in range(PACK, MID_TILES):
            c_tile(j, *first_chunk)
        grouped_4 = regroup_block(4, *first_chunk)
        quantise_wf(0)
        quantise_block(4, grouped_4, *first_chunk)
        transpose_wf(1)
        grouped_5 = regroup_block(5, *first_chunk)
        quantise_wf(1)
        quantise_block(5, grouped_5, *first_chunk)
        quantise_block(6, regroup_block(6, *first_chunk), *first_chunk)

        def prepare_next(index, step):
            if index + 1 == len(CHUNKS):
                return
            following = CHUNKS[index + 1]
            for j in range(C_TILES_A_STEP * (step - FIRST_C_STEP), C_TILES_A_STEP * (step - FIRST_C_STEP + 1)):
                if 0 <= j < MID_TILES:
                    c_tile(j, *following)
            block = step - FIRST_BLOCK_STEP
            if 0 <= block < BLOCKS:
                quantise_block(block, regroup_block(block, *following), *following)

        for index, (col0, width) in enumerate(CHUNKS):
            for half in range(2):
                tiles = range(half * HALF, (half + 1) * HALF)
                y_sums = {}
                for m in tiles:
                    prepare_next(index, 2 * half * HALF + m % HALF)
                    y_sums[m] = sum_banks.tile([P, CHUNK], F32, name="y_sum")
                    y_passes(y_sums[m], m, range(MID_PASSES, FUSED_PASSES), col0, width)
                    if index == 0 and m + WF_AHEAD < OUT_TILES:
                        transpose_wf(m + WF_AHEAD)
                        quantise_wf(m + WF_AHEAD)
                for m in tiles:
                    prepare_next(index, (2 * half + 1) * HALF + m % HALF)
                    y_passes(y_sums[m], m, range(MID_PASSES), col0, width)
                    finish_tile(y_sums[m], m, col0, width)
